import numpy as np
import ml_dtypes


def mxq(x, axis, fmt="e4m3"):
    dtype, down = {"e4m3": (ml_dtypes.float8_e4m3fn, 7), "e5m2": (ml_dtypes.float8_e5m2, 14)}[fmt]
    v = np.moveaxis(np.asarray(x, np.float32).astype(ml_dtypes.bfloat16).astype(np.float64), axis, -1)
    blocks = v.reshape(v.shape[:-1] + (-1, 32))
    amax = np.abs(blocks).max(-1, keepdims=True)
    byte = np.maximum(np.where(amax > 0, np.frexp(amax)[1] - 1 + 127, 0) - down, 1)
    scale = np.exp2(byte - 127.0)
    codes = (blocks / scale).astype(np.float32).astype(dtype).astype(np.float64)
    return np.moveaxis((codes * scale).reshape(v.shape), -1, axis)


WIDE = False


def mx_kscale(k):
    if not WIDE:
        return np.ones(k)
    levels = np.array([10, -10, 5, -5, 0])
    if k % 512:
        return np.exp2(np.random.permutation(np.resize(levels, k // 32))).repeat(32)
    a = np.empty((k // 512, 16))
    for p in range(k // 512):
        a[p, :8] = np.random.permutation(np.resize(levels, 8))
        for g in range(8):
            far = levels[np.abs(levels - a[p, g]) >= 10]
            a[p, g + 8] = far[np.random.randint(len(far))]
    return np.exp2(a.ravel()).repeat(32)


BF16 = ml_dtypes.bfloat16


def bf(x):
    return np.asarray(x, np.float32).astype(BF16)


def f64(x):
    return np.asarray(x).astype(np.float64)


E2M1 = np.array([0.0, 0.5, 1.0, 1.5, 2.0, 3.0, 4.0, 6.0, -0.0, -0.5, -1.0, -1.5, -2.0, -3.0, -4.0, -6.0])


def pack_weight(w, fmt):
    k, n = w.shape
    w = f64(bf(w)).reshape(k // 32, 32, n)
    amax = np.abs(w).max(1)
    if fmt == "e4m3":
        byte = np.frexp(amax)[1] - 1 + 127 - 7
    else:
        mant, ex = np.frexp(amax / 6.0)
        byte = np.where(mant > 0.5, ex, ex - 1) + 127
    byte = np.clip(np.where(amax > 0, byte, 1), 1, 254)
    scaled = (w * np.exp2(127.0 - byte)[:, None, :]).reshape(k, n).astype(np.float32)
    by_word = np.ascontiguousarray(scaled.reshape(k // 512, 128, 4, n).transpose(0, 1, 3, 2))
    if fmt == "e4m3":
        words = by_word.astype(ml_dtypes.float8_e4m3fn).view(np.uint8)
    else:
        c = by_word.astype(ml_dtypes.float4_e2m1fn).view(np.uint8) & 0xF
        words = c[..., 0::2] | (c[..., 1::2] << 4)
    return np.ascontiguousarray(words), np.ascontiguousarray(byte.astype(np.uint8).reshape(k // 512, 16, n))


def unpack_weight(words, scales, fmt):
    g, p, n, _ = words.shape
    if fmt == "e4m3":
        vals = np.ascontiguousarray(words).view(ml_dtypes.float8_e4m3fn).astype(np.float64)
    else:
        nib = np.empty((g, p, n, 4), np.uint8)
        nib[..., 0::2] = words & 0xF
        nib[..., 1::2] = words >> 4
        vals = E2M1[nib]
    vals = vals * np.repeat(np.exp2(scales.astype(np.float64) - 127.0), 8, axis=1)[..., None]
    return vals.transpose(0, 1, 3, 2).reshape(g * 512, n)
def pack4(w):
    words, scales = pack_weight(w, "e2m1")
    return words.reshape(words.shape[0], 128, -1), scales


def unpack4(words, scales):
    return unpack_weight(words.reshape(words.shape[0], 128, -1, 2), scales, "e2m1")


B, C, H, W = 128, 1024, 3, 3
C3, CH, P = 3 * C, C // 2, H * W


def sigmoid(v):
    return 1.0 / (1.0 + np.exp(-v))


def draw0():
    s, t = mx_kscale(C3), mx_kscale(CH)
    n = np.random.standard_normal
    fv = bf(n((B, C3, H, W)) * s[None, :, None, None])
    ft = bf(n((B, C)))
    Wa_words, Wa_scales = pack4((n((CH, C3)) / np.sqrt(C3) / s[None, :] * t[:, None]).T)
    ba = bf(n(CH) * 0.3 * t)
    Wb_words, Wb_scales = pack4((n((C, CH)) * 2.0 / np.sqrt(CH) / t[None, :]).T)
    return {
        "fv": fv,
        "ft": ft,
        "Wa_words": Wa_words,
        "Wa_scales": Wa_scales,
        "ba": ba,
        "Wb_words": Wb_words,
        "Wb_scales": Wb_scales,
        "bb": bf(n(C) * 0.5),
        "Wfc2": bf(n((C, C)) / np.sqrt(C)),
        "bfc2": bf(n(C) * 0.3),
    }


def core(fv, ft, Wa_words, Wa_scales, ba, Wb_words, Wb_scales, bb, Wfc2, bfc2):
    h = np.maximum((unpack4(Wa_words, Wa_scales).T @ mxq(f64(fv).reshape(B, C3, P), 1, "e4m3")) + f64(ba)[None, :, None], 0.0)
    fv2 = (unpack4(Wb_words, Wb_scales).T @ mxq(h, 1, "e4m3")) + f64(bb)[None, :, None]
    gate = sigmoid(fv2.mean(axis=2))
    ft2 = f64(ft) @ f64(Wfc2).T + f64(bfc2)
    return ft2 + ft2 * gate


def e4m3fn_bytes(y):
    return np.clip(np.asarray(y, np.float64), -448.0, 448.0).astype(np.float32).astype(ml_dtypes.float8_e4m3fn).view(np.uint8)


def e4m3fn_values(b):
    return np.asarray(b, np.uint8).view(ml_dtypes.float8_e4m3fn).astype(np.float64)


def setup_inputs():
    d = draw0()
    x0 = np.asarray(d['fv']).astype(np.float64)
    s = (np.max(np.abs(x0), axis=(0, 2, 3), keepdims=True) / 448.0).astype(np.float32)
    out = {}
    for k, v in d.items():
        if k == 'fv':
            out['fv_bytes'] = e4m3fn_bytes(x0 / s.astype(np.float64))
            out['fv_scale'] = s
        else:
            out[k] = v
    return out


def reference(fv_bytes, fv_scale, ft, Wa_words, Wa_scales, ba, Wb_words, Wb_scales, bb, Wfc2, bfc2):
    return core(e4m3fn_values(fv_bytes) * fv_scale.astype(np.float64), ft, Wa_words, Wa_scales, ba, Wb_words, Wb_scales, bb, Wfc2, bfc2)

from contextlib import ExitStack

import concourse.mybir as mybir
from concourse.masks import make_identity

B, C3, C, CH, PIX = 128, 3072, 1024, 512, 9
P = 128
G = C3 // 512
FLOPS = 2 * B * PIX * C3 * CH + 2 * B * PIX * CH * C + 2 * B * C * C

F32 = mybir.dt.float32
BF16 = mybir.dt.bfloat16
I32 = mybir.dt.int32
U32 = mybir.dt.uint32
U8 = mybir.dt.uint8
FP8 = mybir.dt.float8_e4m3fn
FP8X4 = mybir.dt.float8_e4m3fn_x4
FP4X4 = mybir.dt.float4_e2m1fn_x4
ADD = mybir.AluOpType.add
MULT = mybir.AluOpType.mult
ACT = mybir.ActivationFunctionType

GE = 512 * PIX
HALF = GE // 2
ODD_T = 1280
Q_ROW = 2 * (ODD_T + 255)
R_BUFS = 5
XB = 2
EVEN, ODD = 5, 4


def tile_joint_module_pb_w4_kernel(
    tc, fv_bytes, fv_scale, ft, Wa_words, Wa_scales, ba, Wb_words, Wb_scales, bb, Wfc2, bfc2, out
):
    nc = tc.nc
    with ExitStack() as ctx:
        keep = ctx.enter_context(tc.tile_pool(name="keep", bufs=1))
        strm = ctx.enter_context(tc.tile_pool(name="strm", bufs=2))
        psum = ctx.enter_context(tc.psum_pool(name="psum", bufs=1))

        def bank(tag, shape, dtype=F32):
            return psum.tile(shape, dtype, tag=tag, name=tag, bufs=3 if tag == "tp" else 1)

        ctx.enter_context(tc.manual_schedule())

        warm = keep.tile([P, 2], F32)
        nc.vector.memset(warm[:], 0.0)
        nc.scalar.activation(out=warm[:, 1:2], in_=warm[:, 0:1], func=ACT.Sigmoid)
        ident_b = keep.tile([P, P], BF16)
        make_identity(nc, ident_b[:])
        ident_f = keep.tile([P, P], F32)
        make_identity(nc, ident_f[:])
        ones = keep.tile([P, P], BF16)
        nc.gpsimd.memset(ones[:], 1.0)
        row = keep.tile([P, C], BF16)
        nc.gpsimd.memset(row[:], 0.0)
        was = keep.tile([P, G, CH], U8, align_bytes=64)
        wbs = keep.tile([P, C], U8, align_bytes=64)
        nc.gpsimd.memset(was[:].rearrange("p g n -> p (g n)").bitcast(I32), 0)
        nc.gpsimd.memset(wbs[:].bitcast(I32), 0)

        st = keep.tile([P, 4 * G], F32)
        nc.scalar.dma_start(
            out=st[:].rearrange("p (g t) -> p g t", t=4),
            in_=fv_scale.rearrange("o (g p t) h w -> p g (o t h w)", p=P, t=4),
        )
        nc.gpsimd.dma_start(out=row[0:1, :], in_=bfc2.unsqueeze(0))
        fv_flat = fv_bytes.rearrange("b c h w -> b (c h w)")
        fv_tiles = {}

        def load_fv(g, parts):
            size = GE // parts
            for h in range(parts):
                fvb = strm.tile([P, size], U8, name="fvq" if parts == 4 else "fvb", bufs=4 if parts == 4 else 10)
                nc.sync.dma_start(out=fvb[:], in_=fv_flat[:, g * GE + h * size : g * GE + (h + 1) * size])
                fv_tiles[(g, h)] = fvb

        wf_tiles = {}

        def load_wf(i):
            wf = strm.tile([P, C], BF16, name="wf", bufs=8)
            nc.sync.dma_start(out=wf[:], in_=Wfc2[P * i : P * (i + 1), :])
            wf_tiles[i] = wf

        wa = keep.tile([P, G, 2 * CH], U8, align_bytes=64)

        def load_wa(g0, g1):
            nc.sync.dma_start(out=wa[:, g0:g1, :], in_=Wa_words[g0:g1].rearrange("g p n -> p g n"))

        ft_sb = keep.tile([P, C], BF16)

        def load_ft():
            nc.sync.dma_start(out=ft_sb[:], in_=ft)

        was_q = was[:].rearrange("p g n -> p (g n)").bitcast(I32).rearrange("p (g n) -> p g n", g=G)
        wa_s32 = Wa_scales.bitcast(I32).rearrange("g q n -> q g n")
        wbs_q = wbs[:].bitcast(I32)
        wb_s32 = Wb_scales[0].bitcast(I32)
        wb = keep.tile([P, 2 * C], U8, align_bytes=64)
        bat = keep.tile([P, CH], BF16)
        bbt = keep.tile([P, C], BF16)

        def load_scales():
            for q in range(4):
                nc.sync.dma_start(out=was_q[32 * q : 32 * q + 4, :, :], in_=wa_s32[4 * q : 4 * q + 4, :, :])
            for q in range(4):
                nc.sync.dma_start(out=wbs_q[32 * q : 32 * q + 4, :], in_=wb_s32[4 * q : 4 * q + 4, :])

        def load_wb():
            nc.sync.dma_start(out=wb[:], in_=Wb_words[0])

        def load_biases():
            nc.sync.dma_start(out=bat[:], in_=ba.partition_broadcast(P))
            nc.sync.dma_start(out=bbt[:], in_=bb.partition_broadcast(P))

        xb_tiles = {}

        def widen(g, h, engine):
            if g not in xb_tiles:
                xb_tiles[g] = strm.tile([P, GE], BF16, name="xb", bufs=XB)
            part = fv_tiles[(g, h)]
            size = part.shape[1]
            src = part[:].bitcast(FP8)
            dst = xb_tiles[g][:, h * size : (h + 1) * size]
            if engine == "S":
                nc.scalar.copy(out=dst, in_=src)
            else:
                nc.vector.tensor_copy(out=dst, in_=src)

        r_tiles = {}

        tps = {}

        def turn(g, b):
            if g not in r_tiles:
                r_tiles[g] = strm.tile([P, 2 * Q_ROW + 2], BF16, name="rt", bufs=R_BUFS)
            words = [(q, 4) for q in range(2)] if b == 4 else [(b // 2, 5 * (b % 2) + i) for i in range(4)]
            tp = bank("tp", [P, 4, P])
            xw = xb_tiles[g][:].bitcast(F32)
            for i, (q, w) in enumerate(words):
                nc.tensor.transpose(tp[:, i, :], xw[:, 9 * q + w : GE // 2 : 18], ident_f[:])
            tps[(g, b)] = tp

        def evac(g, b, engine):
            tp = tps[(g, b)]
            if b == 4:
                src = tp[:, 0:2, :].rearrange("p w b -> p (w b)").bitcast(BF16).rearrange("p (q b e) -> p q b e", q=2, e=2)
                sc = st[:, 4 * g : 4 * g + 4].rearrange("p (q b e) -> p q b e", q=2, b=1, e=2).to_broadcast([P, 2, P, 2])
                dst = r_tiles[g][:, 0 : 2 * Q_ROW].rearrange("p (q m) -> p q m", q=2)[:, :, 1024 : 1024 + 514]
                dst = dst.rearrange("p q (e l) -> p q l e", e=2)[:, :, 0:256:2, :]
                nc.vector.tensor_tensor(out=dst, in0=src, in1=sc, op=MULT)
                return
            base = (b // 2) * Q_ROW + (b % 2) * (ODD_T + 256)
            src = tp[:].rearrange("p w b -> p (w b)").bitcast(BF16)
            dst = r_tiles[g][:, base : base + 1024]
            scale = st[:, 4 * g + b : 4 * g + b + 1]
            if engine == "S":
                nc.scalar.activation(out=dst, in_=src, func=ACT.Copy, scale=scale)
            else:
                nc.vector.tensor_scalar(out=dst, in0=src, scalar1=scale, scalar2=None, op0=MULT)

        xq = {}

        def interleave(g, odd, engine):
            n = (ODD if odd else EVEN) * P
            x = strm.tile([P, 4 * n], BF16, name="xodd" if odd else "xeven", bufs=3 if odd else 2, align_bytes=64)
            if odd:
                src = r_tiles[g][:, 1 : 1 + 4 * (ODD_T + 255)].rearrange("p (x l) -> p l x", x=4)[:, 0 : 2 * n : 2, :]
                dst = x[:].rearrange("p (k x) -> p k x", x=4)
            else:
                src = r_tiles[g][:, 0 : 2 * Q_ROW].rearrange("p (q m) -> p q m", q=2)[:, :, 0 : 2 * (ODD_T + 1)]
                src = src.rearrange("p q (r l) -> p l q r", r=2)[:, 0 : 2 * n : 2, :, :]
                dst = x[:].rearrange("p (k q r) -> p k q r", q=2, r=2)
            if engine == "S":
                nc.scalar.copy(out=dst, in_=src)
            else:
                nc.vector.tensor_copy(out=dst, in_=src)
            xq[(g, odd)] = x

        codes = {}

        def quantise(g, odd):
            n = (ODD if odd else EVEN) * P
            c = strm.tile([P, n], U32, name="codd" if odd else "ceven", bufs=6 if odd else 3, align_bytes=64)
            s = strm.tile([P, n], U8, name="sodd" if odd else "seven", bufs=6 if odd else 3, align_bytes=64)
            x = xq[(g, odd)]
            for a, b in ((0, 512), (512, 640)):
                if a < n:
                    nc.vector.quantize_mx(out=c[:, a:b].bitcast(FP8X4), scales=s[:, a:b], in_=x[:, 4 * a : 4 * b])
            codes[(g, odd)] = (c, s)

        accs = {}

        def product(g, odd, pixels=None):
            c, s = codes[(g, odd)]
            for i in pixels if pixels is not None else range(ODD if odd else EVEN):
                if g == 0:
                    accs[(odd, i)] = bank("a%d" % i, [P, CH])
                cols = slice(P * i, P * (i + 1))
                nc.tensor.matmul_mx(
                    out=accs[(odd, i)][:],
                    lhsT=c[:, cols].bitcast(FP8X4),
                    lhsT_scale=s[:, cols],
                    rhs=wa[:, g, :].bitcast(FP4X4),
                    rhs_scale=was[:, g, :],
                    start=(g == 0),
                    stop=(g == G - 1),
                )

        hb_tiles = {}

        def add_bias(odd, i):
            hb = strm.tile([P, CH], BF16, name="hb", bufs=4)
            nc.vector.tensor_tensor(out=hb[:], in0=accs[(odd, i)][:], in1=bat[:], op=ADD)
            hb_tiles[(odd, i)] = hb

        xh_tiles = {}

        hts = {}

        def turn_h(odd, pixels):
            n = len(pixels)
            ht = bank("tp", [P, 2, n, P])
            for j, i in enumerate(pixels):
                hw = hb_tiles[(odd, i)][:].bitcast(F32)
                for u in range(2):
                    nc.tensor.transpose(ht[:, u, j, :], hw[:, u : CH // 2 : 2], ident_f[:])
            hts[(odd, pixels)] = ht

        def relu_h(odd, pixels, engine="S"):
            n = len(pixels)
            ht = hts[(odd, pixels)]
            xh = strm.tile([P, n * P * 4], BF16, name="xh", bufs=3, align_bytes=64)
            src = ht[:].rearrange("p u j b -> p (u j b)").bitcast(BF16).rearrange("p (u k e) -> p k u e", u=2, e=2)
            dst = xh[:].rearrange("p (k u e) -> p k u e", u=2, e=2)
            if engine == "S":
                nc.scalar.activation(out=dst, in_=src, func=ACT.Relu)
            else:
                nc.vector.tensor_scalar(out=dst, in0=src, scalar1=0.0, scalar2=None, op0=mybir.AluOpType.max)
            xh_tiles[(odd, pixels)] = xh

        hc_tiles = {}

        def quantise_h(odd, pixels):
            n = len(pixels) * P
            c = strm.tile([P, n], U32, name="hc", bufs=3, align_bytes=64)
            s = strm.tile([P, n], U8, name="hs", bufs=3, align_bytes=64)
            nc.vector.quantize_mx(out=c[:].bitcast(FP8X4), scales=s[:], in_=xh_tiles[(odd, pixels)][:])
            hc_tiles[(odd, pixels)] = (c, s)

        o2 = []

        def product_h(odd, pixels, first=False, last=False):
            if first:
                o2.append(bank("a4", [P, CH]))
                o2.append(bank("tp", [P, CH]))
            for n in range(2):
                for pair in pixels:
                    c, s = hc_tiles[(odd, pair)]
                    for j in range(len(pair)):
                        cols = slice(P * j, P * (j + 1))
                        nc.tensor.matmul_mx(
                            out=o2[n][:],
                            lhsT=c[:, cols].bitcast(FP8X4),
                            lhsT_scale=s[:, cols],
                            rhs=wb[:, 1024 * n : 1024 * (n + 1)].bitcast(FP4X4),
                            rhs_scale=wbs[:, 512 * n : 512 * (n + 1)],
                            start=(first and pair == pixels[0] and j == 0),
                            stop=(last and pair == pixels[-1] and j == len(pair) - 1),
                        )

        ft_t = keep.tile([P, 8, P], BF16)
        wf_t = keep.tile([P, 8, C], BF16)
        ft2 = keep.tile([P, C], F32)

        tws = {}

        def turn_rows(i):
            src = ft_sb if i < 0 else wf_tiles[i]
            tw = bank("a%d" % (2 + (i + 1) % 3), [P, 8, P], BF16)
            for j in range(8):
                nc.tensor.transpose(tw[:, j, :], src[:, P * j : P * (j + 1)], ident_b[:])
            tws[i] = tw

        def copy_rows(i, engine="V"):
            dst = ft_t[:] if i < 0 else wf_t[:, :, P * i : P * (i + 1)]
            if engine == "S":
                nc.scalar.copy(out=dst, in_=tws[i][:])
            else:
                nc.vector.tensor_copy(out=dst, in_=tws[i][:])

        f2 = {}

        def text_product(n):
            cols = slice(512 * n, 512 * (n + 1))
            f2[n] = bank("a%d" % n, [P, CH])
            nc.tensor.matmul(f2[n][:], lhsT=ones[:], rhs=row[:, cols], start=True, stop=False)
            for j in range(8):
                nc.tensor.matmul(f2[n][:], lhsT=ft_t[:, j, :], rhs=wf_t[:, j, cols], start=False, stop=(j == 7))

        def text_out(n, engine):
            cols = slice(512 * n, 512 * (n + 1))
            if engine == "S":
                nc.scalar.copy(out=ft2[:, cols], in_=f2[n][:])
            else:
                nc.vector.tensor_copy(out=ft2[:, cols], in_=f2[n][:])

        zs = {}

        def gate_z(n):
            zs[n] = strm.tile([P, CH], F32, name="z", bufs=2)
            nc.vector.scalar_tensor_tensor(
                out=zs[n][:], in0=o2[n][:], scalar=1.0 / PIX, in1=bbt[:, CH * n : CH * (n + 1)], op0=MULT, op1=ADD
            )

        def gate_s(n):
            nc.scalar.activation(out=zs[n][:], in_=zs[n][:], func=ACT.Sigmoid)

        def gate_o(n):
            cols = slice(CH * n, CH * (n + 1))
            res = strm.tile([P, CH], F32, name="res", bufs=2)
            nc.vector.scalar_tensor_tensor(out=res[:], in0=zs[n][:], scalar=1.0, in1=ft2[:, cols], op0=ADD, op1=MULT)
            nc.sync.dma_start(out=out[:, cols], in_=res[:])

        load_fv(0, 4)
        load_ft()
        load_fv(1, 2)
        load_wf(0)
        turn_rows(-1)
        load_fv(2, 2)
        widen(0, 0, "V")
        widen(0, 2, "V")
        load_wa(3, 6)
        load_wf(3)
        widen(0, 3, "V")
        widen(0, 1, "S")
        turn(0, 1)
        load_wf(4)
        widen(1, 0, "V")
        turn(0, 4)
        load_wa(0, 3)
        evac(0, 1, "V")
        load_wf(6)
        widen(1, 1, "S")
        copy_rows(-1, "S")
        evac(0, 4, "V")
        turn(0, 0)
        evac(0, 0, "V")
        turn(0, 3)
        evac(0, 3, "V")
        turn(0, 2)
        evac(0, 2, "V")
        turn(1, 1)
        evac(1, 1, "V")
        turn(1, 4)
        widen(2, 0, "S")
        turn_rows(0)
        evac(1, 4, "V")
        turn(1, 0)
        turn(1, 3)
        widen(2, 1, "V")
        evac(1, 3, "S")
        turn(1, 2)
        load_wf(5)
        interleave(0, 0, "V")
        turn(2, 1)
        load_wf(1)
        evac(1, 2, "S")
        turn_rows(1)
        evac(1, 0, "S")
        load_fv(3, 2)
        widen(3, 1, "V")
        widen(3, 0, "V")
        turn(2, 0)
        turn(2, 3)
        evac(2, 1, "S")
        copy_rows(0, "S")
        load_wf(2)
        turn_rows(2)
        copy_rows(1, "S")
        evac(2, 3, "S")
        evac(2, 0, "V")
        interleave(1, 0, "V")
        turn(3, 0)
        evac(3, 0, "V")
        turn_rows(3)
        copy_rows(3, "V")
        copy_rows(2, "V")
        turn(2, 4)
        evac(2, 4, "V")
        turn(2, 2)
        quantise(0, 0)
        turn(3, 1)
        turn_rows(6)
        copy_rows(6, "V")
        interleave(1, 1, "S")
        load_fv(5, 2)
        turn_rows(4)
        evac(3, 1, "V")
        turn(3, 4)
        evac(2, 2, "S")
        load_fv(4, 2)
        widen(4, 0, "S")
        quantise(1, 0)
        evac(3, 4, "V")
        text_product(0)
        turn(3, 3)
        turn(3, 2)
        widen(4, 1, "V")
        evac(3, 2, "S")
        turn_rows(5)
        copy_rows(5, "V")
        turn(4, 3)
        evac(3, 3, "V")
        evac(4, 3, "V")
        turn(4, 2)
        quantise(1, 1)
        interleave(0, 1, "V")
        load_wf(7)
        text_out(0, "S")
        copy_rows(4, "S")
        turn_rows(7)
        turn(4, 1)
        evac(4, 2, "S")
        copy_rows(7, "V")
        load_scales()
        widen(5, 1, "V")
        load_biases()
        load_wb()
        turn(4, 4)
        widen(5, 0, "S")
        turn(4, 0)
        evac(4, 0, "S")
        evac(4, 1, "S")
        evac(4, 4, "V")
        text_product(1)
        text_out(1, "S")
        turn(5, 1)
        interleave(2, 0, "V")
        turn(5, 3)
        interleave(4, 0, "S")
        evac(5, 1, "V")
        quantise(2, 0)
        evac(5, 3, "V")
        interleave(3, 0, "V")
        product(0, 0, None)
        turn(5, 2)
        turn(5, 0)
        turn(5, 4)
        evac(5, 4, "V")
        quantise(3, 0)
        evac(5, 0, "S")
        product(1, 0, None)
        quantise(4, 0)
        product(2, 0, None)
        evac(5, 2, "S")
        interleave(5, 0, "V")
        quantise(5, 0)
        interleave(3, 1, "S")
        interleave(2, 1, "S")
        quantise(0, 1)
        product(3, 0, None)
        product(4, 0, None)
        product(5, 0, None)
        add_bias(0, 0)
        add_bias(0, 1)
        turn_h(0, (0, 1))
        add_bias(0, 2)
        add_bias(0, 3)
        product(0, 1, (0, 1))
        quantise(2, 1)
        interleave(4, 1, "S")
        quantise(3, 1)
        product(1, 1, (0, 1))
        product(0, 1, (2, 3))
        relu_h(0, (0, 1), "S")
        add_bias(0, 4)
        product(1, 1, (2, 3))
        quantise(4, 1)
        turn_h(0, (2, 3))
        relu_h(0, (2, 3), "V")
        interleave(5, 1, "V")
        quantise(5, 1)
        turn_h(0, (4,))
        relu_h(0, (4,), "S")
        quantise_h(0, (0, 1))
        product(2, 1, None)
        product(3, 1, None)
        quantise_h(0, (2, 3))
        product(4, 1, None)
        product(5, 1, None)
        quantise_h(0, (4,))
        product_h(0, ((4,),), True, False)
        add_bias(1, 0)
        add_bias(1, 1)
        add_bias(1, 3)
        add_bias(1, 2)
        product_h(0, ((0, 1),), False, False)
        turn_h(1, (0, 1))
        relu_h(1, (0, 1), "V")
        quantise_h(1, (0, 1))
        turn_h(1, (2, 3))
        relu_h(1, (2, 3), "V")
        quantise_h(1, (2, 3))
        product_h(0, ((2, 3),), False, False)
        product_h(1, ((0, 1), (2, 3)), False, True)
        gate_z(0)
        gate_s(0)
        gate_z(1)
        gate_o(0)
        gate_s(1)
        gate_o(1)
